import numpy as np
import ml_dtypes


def mxq(x, axis, fmt="e4m3"):
    dtype, down = {"e4m3": (ml_dtypes.float8_e4m3fn, 7), "e5m2": (ml_dtypes.float8_e5m2, 14)}[fmt]
    v = np.moveaxis(np.asarray(x, np.float32).astype(ml_dtypes.bfloat16).astype(np.float64), axis, -1)
    blocks = v.reshape(v.shape[:-1] + (-1, 32))
    amax = np.abs(blocks).max(-1, keepdims=True)
    byte = np.maximum(np.where(amax > 0, np.frexp(amax)[1] - 1 + 127, 0) - down, 1)
    scale = np.exp2(byte - 127.0)
    codes = (blocks / scale).astype(np.float32).astype(dtype).astype(np.float64)
    return np.moveaxis((codes * scale).reshape(v.shape), -1, axis)


WIDE = False


def mx_kscale(k):
    if not WIDE:
        return np.ones(k)
    levels = np.array([10, -10, 5, -5, 0])
    if k % 512:
        return np.exp2(np.random.permutation(np.resize(levels, k // 32))).repeat(32)
    a = np.empty((k // 512, 16))
    for p in range(k // 512):
        a[p, :8] = np.random.permutation(np.resize(levels, 8))
        for g in range(8):
            far = levels[np.abs(levels - a[p, g]) >= 10]
            a[p, g + 8] = far[np.random.randint(len(far))]
    return np.exp2(a.ravel()).repeat(32)


BF16 = ml_dtypes.bfloat16


def bf(x):
    return np.asarray(x, np.float32).astype(BF16)


def f64(x):
    return np.asarray(x).astype(np.float64)


B, D, I, O = 4096, 4, 512, 256


def setup_inputs():
    s = np.tile(mx_kscale(I), D)
    return {"x": bf(np.random.standard_normal((B, D * I)) * s),
            "W": bf(np.random.standard_normal((D * O, D * I)) / np.sqrt(I) / s[None, :])}


def reference(x, W):
    W4 = f64(W).reshape(D, O, D, I)
    Wb = np.ascontiguousarray(np.einsum('dodi->doi', W4))
    xb = f64(x).reshape(B, D, I)
    xq = mxq(xb, 2, "e4m3")
    wq = mxq(Wb, 2, "e4m3")
    out = xq.transpose(1, 0, 2) @ wq.transpose(0, 2, 1)
    return out.transpose(1, 0, 2).reshape(B, D * O)

@@ -1,0 +1,178 @@
+from contextlib import ExitStack
+
+import concourse.mybir as mybir
+from concourse.masks import make_identity
+
+FP8X4 = mybir.dt.float8_e4m3fn_x4
+BF16 = mybir.dt.bfloat16
+F32 = mybir.dt.float32
+U32 = mybir.dt.uint32
+U8 = mybir.dt.uint8
+
+P = 128
+B, D, I, O = 4096, 4, 512, 256
+ROW_TILES = B // P
+XW = D * I
+OW = D * O
+ROW_BYTES = 4096
+
+FLOPS = 2 * B * D * I * O
+BYTES = B * XW * 2 + D * O * I * 2 + B * OW * 4
+
+X_CHUNKS = (1, 1, 2, 4, 8, 8, 8)
+OUT_CHUNKS = ((1,), (1,), (2,), (4,), (4, 4), (4, 4), (4, 2, 1, 1))
+LAG = 8
+GROUP = 2
+
+
+def tile_ensemblelinear_t_kernel(tc, x, W, out):
+    nc = tc.nc
+    with ExitStack() as ctx:
+        const = ctx.enter_context(tc.tile_pool(name="const", bufs=1))
+        xo = ctx.enter_context(tc.tile_pool(name="xo", bufs=1))
+        work = ctx.enter_context(tc.tile_pool(name="work", bufs=4))
+        psum = ctx.enter_context(tc.psum_pool(name="psum", bufs=4))
+        ctx.enter_context(tc.manual_schedule())
+
+        ident = const.tile([P, P], F32, name="ident")
+        make_identity(nc, ident[:])
+
+        w_sb = const.tile([P, D * 2 * I], BF16, name="w_sb")
+        for d in range(D):
+            nc.sync.dma_start(
+                out=w_sb[:, d * 2 * I : (d + 1) * 2 * I].rearrange("p (h k) -> p h k", h=2),
+                in_=W[d * O : (d + 1) * O, d * I : (d + 1) * I].rearrange("(h p) k -> p h k", p=P),
+            )
+        x_words = []
+        first = 0
+        for c, t_rows in enumerate(X_CHUNKS):
+            xc = xo.tile([P, t_rows * XW], BF16, name="x%d" % c, offset=(LAG + first) * ROW_BYTES)
+            nc.sync.dma_start(
+                out=xc[:],
+                in_=x[first * P : (first + t_rows) * P, :].rearrange("(p t) k -> p (t k)", t=t_rows),
+            )
+            xw = xc[:].bitcast(F32)
+            for j in range(t_rows):
+                x_words.append(xw[:, j * (XW // 2) : (j + 1) * (XW // 2)])
+            first += t_rows
+
+        w_words = w_sb[:].bitcast(F32)
+        w_grouped = const.tile([P, D * O * 4], BF16, name="w_grouped", align_bytes=64)
+        w_gw = w_grouped[:].bitcast(F32)
+        w_codes = const.tile([P, D * O], U32, name="w_codes", align_bytes=64)
+        w_scales = const.tile([P, D * O], U8, name="w_scales", align_bytes=64)
+        for d in range(D):
+            wt = psum.tile([P, 512], F32, name="wt", tag="acc")
+            for u in range(2):
+                for h in range(2):
+                    nc.tensor.transpose(
+                        wt[:, u * 256 + h * 128 : u * 256 + h * 128 + 128],
+                        w_words[:, d * 512 + h * 256 + u : d * 512 + (h + 1) * 256 : 2],
+                        ident[:],
+                    )
+            dst = w_gw[:, d * 512 : (d + 1) * 512].rearrange("p (o u) -> p o u", u=2)
+            src = wt[:].rearrange("p (u o) -> p o u", u=2)
+            if d < 2:
+                nc.vector.tensor_copy(out=dst, in_=src)
+            else:
+                nc.scalar.copy(out=dst, in_=src)
+
+        banks = {}
+        grouped = {}
+        codes = {}
+        scales = {}
+        accs = {}
+
+        def transposes(g):
+            for i in range(g * GROUP, (g + 1) * GROUP):
+                for b in range(2):
+                    xt = psum.tile([P, 512], F32, name="xt", tag="xt")
+                    banks[(i, b)] = xt
+                    for q in range(4):
+                        d, u = 2 * b + q // 2, q % 2
+                        nc.tensor.transpose(
+                            xt[:, q * 128 : (q + 1) * 128],
+                            x_words[i][:, d * 256 + u : (d + 1) * 256 : 2],
+                            ident[:],
+                        )
+
+        def regroup(g):
+            n = 0
+            for i in range(g * GROUP, (g + 1) * GROUP):
+                gr = work.tile([P, XW], BF16, name="gr", tag="gr", align_bytes=64)
+                grouped[i] = gr
+                gw = gr[:].bitcast(F32)
+                for b in range(2):
+                    dst = gw[:, b * 512 : (b + 1) * 512].rearrange("p (d r u) -> p d r u", d=2, u=2)
+                    src = banks[(i, b)][:].rearrange("p (d u r) -> p d r u", d=2, u=2)
+                    if n < 2 * GROUP - 1:
+                        nc.vector.tensor_copy(out=dst, in_=src)
+                    else:
+                        nc.scalar.copy(out=dst, in_=src)
+                    n += 1
+
+        def quantise(g):
+            for i in range(g * GROUP, (g + 1) * GROUP):
+                cd = work.tile([P, XW // 4], U32, name="cd", tag="cd", align_bytes=64)
+                sc = work.tile([P, XW // 4], U8, name="sc", tag="sc", align_bytes=64)
+                codes[i] = cd
+                scales[i] = sc
+                nc.vector.quantize_mx(out=cd[:].bitcast(FP8X4), scales=sc[:], in_=grouped[i][:])
+
+        def multiply(g):
+            for i in range(g * GROUP, (g + 1) * GROUP):
+                for b in range(2):
+                    acc = psum.tile([P, 512], F32, name="acc", tag="acc")
+                    accs[(i, b)] = acc
+                    for e in range(2):
+                        d = 2 * b + e
+                        nc.tensor.matmul_mx(
+                            out=acc[:, e * O : (e + 1) * O],
+                            lhsT=codes[i][:, d * P : (d + 1) * P].bitcast(FP8X4),
+                            lhsT_scale=scales[i][:, d * P : (d + 1) * P],
+                            rhs=w_codes[:, d * O : (d + 1) * O].bitcast(FP8X4),
+                            rhs_scale=w_scales[:, d * O : (d + 1) * O],
+                            start=True,
+                            stop=True,
+                        )
+
+        plan = {}
+        first = 0
+        for c, t_rows in enumerate(X_CHUNKS):
+            view = out[first * P : (first + t_rows) * P, :].rearrange("(p t) n -> p t n", t=t_rows)
+            s = 0
+            for n_rows in OUT_CHUNKS[c]:
+                for j in range(n_rows):
+                    plan[first + s + j] = (first + s, n_rows, j, view[:, s : s + n_rows, :])
+                s += n_rows
+            first += t_rows
+        out_tiles = {}
+
+        def drain(g):
+            for i in range(g * GROUP, (g + 1) * GROUP):
+                start_tile, n_rows, j, view = plan[i]
+                if j == 0:
+                    out_tiles[start_tile] = xo.tile(
+                        [P, n_rows * OW], F32, name="o%d" % start_tile, offset=start_tile * ROW_BYTES
+                    )
+                ot = out_tiles[start_tile]
+                for b in range(2):
+                    nc.scalar.copy(
+                        out=ot[:, j * OW + b * 512 : j * OW + (b + 1) * 512], in_=accs[(i, b)][:]
+                    )
+                if j == n_rows - 1:
+                    nc.sync.dma_start(out=view, in_=ot[:].rearrange("p (t n) -> p t n", t=n_rows))
+
+        groups = ROW_TILES // GROUP
+        transposes(0)
+        regroup(0)
+        nc.vector.quantize_mx(out=w_codes[:].bitcast(FP8X4), scales=w_scales[:], in_=w_grouped[:])
+        quantise(0)
+        for g in range(groups):
+            if g + 1 < groups:
+                transposes(g + 1)
+                regroup(g + 1)
+            multiply(g)
+            if g + 1 < groups:
+                quantise(g + 1)
+            drain(g)

@@ -19,8 +19,8 @@ ROW_BYTES = 4096
 FLOPS = 2 * B * D * I * O
 BYTES = B * XW * 2 + D * O * I * 2 + B * OW * 4
 
-X_CHUNKS = (1, 1, 2, 4, 8, 8, 8)
-OUT_CHUNKS = ((1,), (1,), (2,), (4,), (4, 4), (4, 4), (4, 2, 1, 1))
+X_CHUNKS = (2, 6, 8, 8, 8)
+OUT_CHUNKS = ((2,), (6,), (8,), (8,), (4, 4))
 LAG = 8
 GROUP = 2
 

@@ -37,7 +37,7 @@ def tile_ensemblelinear_t_kernel(tc, x, W, out):
         ident = const.tile([P, P], F32, name="ident")
         make_identity(nc, ident[:])
 
-        w_sb = const.tile([P, D * 2 * I], BF16, name="w_sb")
+        w_sb = const.tile([P, D * 2 * I], BF16, name="w_sb", align_bytes=256)
         for d in range(D):
             nc.sync.dma_start(
                 out=w_sb[:, d * 2 * I : (d + 1) * 2 * I].rearrange("p (h k) -> p h k", h=2),
@@ -46,7 +46,7 @@ def tile_ensemblelinear_t_kernel(tc, x, W, out):
         x_words = []
         first = 0
         for c, t_rows in enumerate(X_CHUNKS):
-            xc = xo.tile([P, t_rows * XW], BF16, name="x%d" % c, offset=(LAG + first) * ROW_BYTES)
+            xc = xo.tile([P, t_rows * XW], BF16, name="x%d" % c, offset=(LAG + first) * ROW_BYTES, align_bytes=256)
             nc.sync.dma_start(
                 out=xc[:],
                 in_=x[first * P : (first + t_rows) * P, :].rearrange("(p t) k -> p (t k)", t=t_rows),
@@ -153,7 +153,7 @@ def tile_ensemblelinear_t_kernel(tc, x, W, out):
                 start_tile, n_rows, j, view = plan[i]
                 if j == 0:
                     out_tiles[start_tile] = xo.tile(
-                        [P, n_rows * OW], F32, name="o%d" % start_tile, offset=start_tile * ROW_BYTES
+                        [P, n_rows * OW], F32, name="o%d" % start_tile, offset=start_tile * ROW_BYTES, align_bytes=256
                     )
                 ot = out_tiles[start_tile]
                 for b in range(2):

@@ -19,8 +19,8 @@ ROW_BYTES = 4096
 FLOPS = 2 * B * D * I * O
 BYTES = B * XW * 2 + D * O * I * 2 + B * OW * 4
 
-X_CHUNKS = (2, 6, 8, 8, 8)
-OUT_CHUNKS = ((2,), (6,), (8,), (8,), (4, 4))
+X_CHUNKS = (4, 4, 8, 8, 8)
+OUT_CHUNKS = ((4,), (4,), (8,), (8,), (4, 4))
 LAG = 8
 GROUP = 2
 

from contextlib import ExitStack

import concourse.mybir as mybir
from concourse.masks import make_identity

FP8X4 = mybir.dt.float8_e4m3fn_x4
BF16 = mybir.dt.bfloat16
F32 = mybir.dt.float32
U32 = mybir.dt.uint32
U8 = mybir.dt.uint8

P = 128
B, D, I, O = 4096, 4, 512, 256
ROW_TILES = B // P
XW = D * I
OW = D * O
ROW_BYTES = 4096

FLOPS = 2 * B * D * I * O
BYTES = B * XW * 2 + D * O * I * 2 + B * OW * 4

X_CHUNKS = (4, 4, 8, 8, 8)
OUT_CHUNKS = ((4,), (4,), (8,), (8,), (4, 4))
LAG = 8
GROUP = 2


def tile_ensemblelinear_t_kernel(tc, x, W, out):
    nc = tc.nc
    with ExitStack() as ctx:
        const = ctx.enter_context(tc.tile_pool(name="const", bufs=1))
        xo = ctx.enter_context(tc.tile_pool(name="xo", bufs=1))
        work = ctx.enter_context(tc.tile_pool(name="work", bufs=4))
        psum = ctx.enter_context(tc.psum_pool(name="psum", bufs=4))
        ctx.enter_context(tc.manual_schedule())

        ident = const.tile([P, P], F32, name="ident")
        make_identity(nc, ident[:])

        w_sb = const.tile([P, D * 2 * I], BF16, name="w_sb", align_bytes=256)
        for d in range(D):
            nc.sync.dma_start(
                out=w_sb[:, d * 2 * I : (d + 1) * 2 * I].rearrange("p (h k) -> p h k", h=2),
                in_=W[d * O : (d + 1) * O, d * I : (d + 1) * I].rearrange("(h p) k -> p h k", p=P),
            )
        x_words = []
        first = 0
        for c, t_rows in enumerate(X_CHUNKS):
            xc = xo.tile([P, t_rows * XW], BF16, name="x%d" % c, offset=(LAG + first) * ROW_BYTES, align_bytes=256)
            nc.sync.dma_start(
                out=xc[:],
                in_=x[first * P : (first + t_rows) * P, :].rearrange("(p t) k -> p (t k)", t=t_rows),
            )
            xw = xc[:].bitcast(F32)
            for j in range(t_rows):
                x_words.append(xw[:, j * (XW // 2) : (j + 1) * (XW // 2)])
            first += t_rows

        w_words = w_sb[:].bitcast(F32)
        w_grouped = const.tile([P, D * O * 4], BF16, name="w_grouped", align_bytes=64)
        w_gw = w_grouped[:].bitcast(F32)
        w_codes = const.tile([P, D * O], U32, name="w_codes", align_bytes=64)
        w_scales = const.tile([P, D * O], U8, name="w_scales", align_bytes=64)
        for d in range(D):
            wt = psum.tile([P, 512], F32, name="wt", tag="acc")
            for u in range(2):
                for h in range(2):
                    nc.tensor.transpose(
                        wt[:, u * 256 + h * 128 : u * 256 + h * 128 + 128],
                        w_words[:, d * 512 + h * 256 + u : d * 512 + (h + 1) * 256 : 2],
                        ident[:],
                    )
            dst = w_gw[:, d * 512 : (d + 1) * 512].rearrange("p (o u) -> p o u", u=2)
            src = wt[:].rearrange("p (u o) -> p o u", u=2)
            if d < 2:
                nc.vector.tensor_copy(out=dst, in_=src)
            else:
                nc.scalar.copy(out=dst, in_=src)

        banks = {}
        grouped = {}
        codes = {}
        scales = {}
        accs = {}

        def transposes(g):
            for i in range(g * GROUP, (g + 1) * GROUP):
                for b in range(2):
                    xt = psum.tile([P, 512], F32, name="xt", tag="xt")
                    banks[(i, b)] = xt
                    for q in range(4):
                        d, u = 2 * b + q // 2, q % 2
                        nc.tensor.transpose(
                            xt[:, q * 128 : (q + 1) * 128],
                            x_words[i][:, d * 256 + u : (d + 1) * 256 : 2],
                            ident[:],
                        )

        def regroup(g):
            n = 0
            for i in range(g * GROUP, (g + 1) * GROUP):
                gr = work.tile([P, XW], BF16, name="gr", tag="gr", align_bytes=64)
                grouped[i] = gr
                gw = gr[:].bitcast(F32)
                for b in range(2):
                    dst = gw[:, b * 512 : (b + 1) * 512].rearrange("p (d r u) -> p d r u", d=2, u=2)
                    src = banks[(i, b)][:].rearrange("p (d u r) -> p d r u", d=2, u=2)
                    if n < 2 * GROUP - 1:
                        nc.vector.tensor_copy(out=dst, in_=src)
                    else:
                        nc.scalar.copy(out=dst, in_=src)
                    n += 1

        def quantise(g):
            for i in range(g * GROUP, (g + 1) * GROUP):
                cd = work.tile([P, XW // 4], U32, name="cd", tag="cd", align_bytes=64)
                sc = work.tile([P, XW // 4], U8, name="sc", tag="sc", align_bytes=64)
                codes[i] = cd
                scales[i] = sc
                nc.vector.quantize_mx(out=cd[:].bitcast(FP8X4), scales=sc[:], in_=grouped[i][:])

        def multiply(g):
            for i in range(g * GROUP, (g + 1) * GROUP):
                for b in range(2):
                    acc = psum.tile([P, 512], F32, name="acc", tag="acc")
                    accs[(i, b)] = acc
                    for e in range(2):
                        d = 2 * b + e
                        nc.tensor.matmul_mx(
                            out=acc[:, e * O : (e + 1) * O],
                            lhsT=codes[i][:, d * P : (d + 1) * P].bitcast(FP8X4),
                            lhsT_scale=scales[i][:, d * P : (d + 1) * P],
                            rhs=w_codes[:, d * O : (d + 1) * O].bitcast(FP8X4),
                            rhs_scale=w_scales[:, d * O : (d + 1) * O],
                            start=True,
                            stop=True,
                        )

        plan = {}
        first = 0
        for c, t_rows in enumerate(X_CHUNKS):
            view = out[first * P : (first + t_rows) * P, :].rearrange("(p t) n -> p t n", t=t_rows)
            s = 0
            for n_rows in OUT_CHUNKS[c]:
                for j in range(n_rows):
                    plan[first + s + j] = (first + s, n_rows, j, view[:, s : s + n_rows, :])
                s += n_rows
            first += t_rows
        out_tiles = {}

        def drain(g):
            for i in range(g * GROUP, (g + 1) * GROUP):
                start_tile, n_rows, j, view = plan[i]
                if j == 0:
                    out_tiles[start_tile] = xo.tile(
                        [P, n_rows * OW], F32, name="o%d" % start_tile, offset=start_tile * ROW_BYTES, align_bytes=256
                    )
                ot = out_tiles[start_tile]
                for b in range(2):
                    nc.scalar.copy(
                        out=ot[:, j * OW + b * 512 : j * OW + (b + 1) * 512], in_=accs[(i, b)][:]
                    )
                if j == n_rows - 1:
                    nc.sync.dma_start(out=view, in_=ot[:].rearrange("p (t n) -> p t n", t=n_rows))

        groups = ROW_TILES // GROUP
        transposes(0)
        regroup(0)
        nc.vector.quantize_mx(out=w_codes[:].bitcast(FP8X4), scales=w_scales[:], in_=w_grouped[:])
        quantise(0)
        for g in range(groups):
            if g + 1 < groups:
                transposes(g + 1)
                regroup(g + 1)
            multiply(g)
            if g + 1 < groups:
                quantise(g + 1)
            drain(g)
